import numpy as np
import ml_dtypes


def mxq(x, axis, fmt="e4m3"):
    dtype, down = {"e4m3": (ml_dtypes.float8_e4m3fn, 7), "e5m2": (ml_dtypes.float8_e5m2, 14)}[fmt]
    v = np.moveaxis(np.asarray(x, np.float32).astype(ml_dtypes.bfloat16).astype(np.float64), axis, -1)
    blocks = v.reshape(v.shape[:-1] + (-1, 32))
    amax = np.abs(blocks).max(-1, keepdims=True)
    byte = np.maximum(np.where(amax > 0, np.frexp(amax)[1] - 1 + 127, 0) - down, 1)
    scale = np.exp2(byte - 127.0)
    codes = (blocks / scale).astype(np.float32).astype(dtype).astype(np.float64)
    return np.moveaxis((codes * scale).reshape(v.shape), -1, axis)


WIDE = False


def mx_kscale(k):
    if not WIDE:
        return np.ones(k)
    levels = np.array([10, -10, 5, -5, 0])
    a = np.random.permutation(np.resize(levels, k // 512 * 4)).reshape(k // 512, 4)
    idx = np.arange(k)
    return np.exp2(a[idx // 512, idx % 128 // 32])


BF16 = ml_dtypes.bfloat16


def bf(x):
    return np.asarray(x, np.float32).astype(BF16)


def f64(x):
    return np.asarray(x).astype(np.float64)


E2M1 = np.array([0.0, 0.5, 1.0, 1.5, 2.0, 3.0, 4.0, 6.0, -0.0, -0.5, -1.0, -1.5, -2.0, -3.0, -4.0, -6.0])


def pack_weight(w, fmt):
    k, n = w.shape
    w = f64(bf(w)).reshape(k // 32, 32, n)
    amax = np.abs(w).max(1)
    if fmt == "e4m3":
        byte = np.frexp(amax)[1] - 1 + 127 - 7
    else:
        mant, ex = np.frexp(amax / 6.0)
        byte = np.where(mant > 0.5, ex, ex - 1) + 127
    byte = np.clip(np.where(amax > 0, byte, 1), 1, 254)
    scaled = (w * np.exp2(127.0 - byte)[:, None, :]).reshape(k, n).astype(np.float32)
    by_word = np.ascontiguousarray(scaled.reshape(k // 512, 128, 4, n).transpose(0, 1, 3, 2))
    if fmt == "e4m3":
        words = by_word.astype(ml_dtypes.float8_e4m3fn).view(np.uint8)
    else:
        c = by_word.astype(ml_dtypes.float4_e2m1fn).view(np.uint8) & 0xF
        words = c[..., 0::2] | (c[..., 1::2] << 4)
    return np.ascontiguousarray(words), np.ascontiguousarray(byte.astype(np.uint8).reshape(k // 512, 16, n))


def unpack_weight(words, scales, fmt):
    g, p, n, _ = words.shape
    if fmt == "e4m3":
        vals = np.ascontiguousarray(words).view(ml_dtypes.float8_e4m3fn).astype(np.float64)
    else:
        nib = np.empty((g, p, n, 4), np.uint8)
        nib[..., 0::2] = words & 0xF
        nib[..., 1::2] = words >> 4
        vals = E2M1[nib]
    vals = vals * np.repeat(np.exp2(scales.astype(np.float64) - 127.0), 8, axis=1)[..., None]
    return vals.transpose(0, 1, 3, 2).reshape(g * 512, n)


B, S, D, E, R = 2, 1024, 4096, 8, 64


def setup_inputs():
    s = mx_kscale(D)
    x = bf(np.random.standard_normal((B, S, D)) * s)
    W = np.random.standard_normal((E, R, D)) * (1.0 / np.sqrt(D)) / s
    cat = np.ascontiguousarray(W.swapaxes(1, 2)).reshape(-1, R)
    words, scales = pack_weight(cat, "e4m3")
    return {"x": x, "W_words": words, "W_scales": scales}


def reference(x, W_words, W_scales):
    xq = mxq(f64(x), 2, "e4m3")
    Wt = unpack_weight(W_words, W_scales, "e4m3").reshape(E, D, R)
    y = xq[None, :, :, :] @ Wt[:, None, :, :]
    return tuple(y[e] for e in range(E))

@@ -1,0 +1,164 @@
+from contextlib import ExitStack
+
+import concourse.mybir as mybir
+from concourse.masks import make_identity
+
+FP8X4 = mybir.dt.float8_e4m3fn_x4
+BF16 = mybir.dt.bfloat16
+F32 = mybir.dt.float32
+I32 = mybir.dt.int32
+U32 = mybir.dt.uint32
+U8 = mybir.dt.uint8
+
+P = 128
+PACK = 4
+K_PASS = P * PACK
+TOKENS = 2 * 1024
+D = 4096
+EXPERTS = 8
+RANK = 64
+N_ALL = EXPERTS * RANK
+PASSES = D // K_PASS
+TILES = TOKENS // P
+WORDS_PASS = K_PASS // 2
+PASSES_BANK = 2
+BANKS_TILE = PASSES // PASSES_BANK
+PASSES_QUANT = 4
+X_BUFS = 8
+X_FIRST = 2
+STORE_TILES = 4
+
+FLOPS = 2 * TOKENS * D * N_ALL
+
+
+def tile_moelineara_e_kernel(tc, x, W_words, W_scales, *outs):
+    nc = tc.nc
+
+    x_tiles = x.flatten_outer_dims().rearrange("(p j) k -> p j k", j=TILES)
+    out_tiles = [o.flatten_outer_dims().rearrange("(p j) r -> p j r", j=TILES) for o in outs]
+    w_words_by_pass = W_words.rearrange("(e g) p n t -> g p e (n t)", g=PASSES)
+
+    with ExitStack() as ctx:
+        keep = ctx.enter_context(tc.tile_pool(name="keep", bufs=1))
+        x_pool = ctx.enter_context(tc.tile_pool(name="x_pool", bufs=X_BUFS))
+        grouped_pool = ctx.enter_context(tc.tile_pool(name="grouped_pool", bufs=2))
+        quant_pool = ctx.enter_context(tc.tile_pool(name="quant_pool", bufs=3))
+        res_pool = ctx.enter_context(tc.tile_pool(name="res_pool", bufs=2))
+        psum_t = ctx.enter_context(tc.psum_pool(name="psum_t", bufs=BANKS_TILE))
+        psum_acc = ctx.enter_context(tc.psum_pool(name="psum_acc", bufs=4))
+        ctx.enter_context(tc.manual_schedule())
+
+        x_raw = {}
+        x_codes = {}
+        x_planes = {}
+        results = {}
+
+        def load_x(j):
+            x_raw[j] = x_pool.tile([P, D], BF16, name="x_raw")
+            nc.sync.dma_start(out=x_raw[j][:], in_=x_tiles[:, j, :])
+
+        def transpose_tile(j):
+            words = x_raw[j][:].bitcast(F32)
+            grouped = grouped_pool.tile([P, PASSES, P, PACK], BF16, name="grouped", align_bytes=64)
+            grouped_words = grouped[:].bitcast(F32)
+            for b in range(BANKS_TILE):
+                planes = psum_t.tile([P, PASSES_BANK, 2, P], F32, name="planes")
+                for a in range(PASSES_BANK):
+                    first = (b * PASSES_BANK + a) * WORDS_PASS
+                    for u in range(2):
+                        nc.tensor.transpose(
+                            planes[:, a, u, :],
+                            words[:, first + u : first + WORDS_PASS : 2],
+                            identity[:],
+                        )
+                nc.scalar.copy(
+                    out=grouped_words[:, b * PASSES_BANK : (b + 1) * PASSES_BANK, :, :],
+                    in_=planes[:].rearrange("p a u r -> p a r u"),
+                )
+            return grouped
+
+        def quantise_tile(j, grouped):
+            x_codes[j] = quant_pool.tile([P, PASSES, P], U32, name="x_codes", align_bytes=64)
+            x_planes[j] = quant_pool.tile([P, PASSES, P], U8, name="x_planes", align_bytes=64)
+            for g in range(0, PASSES, PASSES_QUANT):
+                some = slice(g, g + PASSES_QUANT)
+                nc.vector.quantize_mx(
+                    out=x_codes[j][:, some, :].rearrange("p g r -> p (g r)").bitcast(FP8X4),
+                    scales=x_planes[j][:, some, :].rearrange("p g r -> p (g r)"),
+                    in_=grouped[:, some, :, :].rearrange("p g r t -> p (g r t)"),
+                )
+
+        def multiply_tile(j):
+            acc = psum_acc.tile([P, N_ALL], F32, name="acc")
+            for g in range(PASSES):
+                nc.tensor.matmul_mx(
+                    out=acc[:],
+                    lhsT=x_codes[j][:, g, :].bitcast(FP8X4),
+                    lhsT_scale=x_planes[j][:, g, :],
+                    rhs=w_codes[:, g, :].bitcast(FP8X4),
+                    rhs_scale=w_planes[:, g, :],
+                    start=(g == 0),
+                    stop=(g == PASSES - 1),
+                )
+            return acc
+
+        def store_tile(j, acc):
+            group, i = divmod(j, STORE_TILES)
+            if i == 0:
+                results[group] = res_pool.tile([P, EXPERTS, STORE_TILES, RANK], F32, name="results")
+            nc.vector.tensor_copy(
+                out=results[group][:, :, i, :],
+                in_=acc[:].rearrange("p (e r) -> p e r", e=EXPERTS),
+            )
+            if i == STORE_TILES - 1:
+                for e in range(EXPERTS):
+                    nc.sync.dma_start(
+                        out=out_tiles[e][:, group * STORE_TILES : (group + 1) * STORE_TILES, :],
+                        in_=results[group][:, e, :, :],
+                    )
+
+        identity = keep.tile([P, P], F32, name="identity")
+        make_identity(nc, identity[:])
+
+        w_planes_by_group = keep.tile([P, EXPERTS * PASSES, RANK], U8, name="w_planes_by_group")
+        nc.vector.memset(w_planes_by_group[:].bitcast(I32), 0)
+        for quadrant in range(4):
+            nc.gpsimd.dma_start(
+                out=w_planes_by_group[32 * quadrant : 32 * quadrant + 4, :, :].bitcast(F32),
+                in_=W_scales[:, 4 * quadrant : 4 * quadrant + 4, :]
+                .rearrange("c r n -> r c n")
+                .bitcast(F32),
+            )
+
+        for j in range(X_FIRST):
+            load_x(j)
+
+        w_codes = keep.tile([P, PASSES, N_ALL], U32, name="w_codes", align_bytes=64)
+        for g in range(PASSES):
+            nc.sync.dma_start(
+                out=w_codes[:, g, :].bitcast(I32).rearrange("p (e n) -> p e n", e=EXPERTS),
+                in_=w_words_by_pass[g].bitcast(I32),
+            )
+
+        for j in range(X_FIRST, X_BUFS):
+            load_x(j)
+
+        grouped_next = transpose_tile(0)
+        load_x(X_BUFS)
+        quantise_tile(0, grouped_next)
+
+        w_planes = keep.tile([P, PASSES, N_ALL], U8, name="w_planes", align_bytes=64)
+        nc.vector.tensor_copy(
+            out=w_planes[:].bitcast(I32).rearrange("p g (e n) -> p g e n", e=EXPERTS),
+            in_=w_planes_by_group[:].bitcast(I32).rearrange("p (e g) n -> p g e n", g=PASSES),
+        )
+
+        for j in range(TILES):
+            if j + 1 < TILES:
+                grouped_next = transpose_tile(j + 1)
+            if j + 1 + X_BUFS < TILES:
+                load_x(j + 1 + X_BUFS)
+            acc = multiply_tile(j)
+            if j + 1 < TILES:
+                quantise_tile(j + 1, grouped_next)
+            store_tile(j, acc)

@@ -20,7 +20,6 @@ RANK = 64
 N_ALL = EXPERTS * RANK
 PASSES = D // K_PASS
 TILES = TOKENS // P
-WORDS_PASS = K_PASS // 2
 PASSES_BANK = 2
 BANKS_TILE = PASSES // PASSES_BANK
 PASSES_QUANT = 4
@@ -41,6 +40,7 @@ def tile_moelineara_e_kernel(tc, x, W_words, W_scales, *outs):
     with ExitStack() as ctx:
         keep = ctx.enter_context(tc.tile_pool(name="keep", bufs=1))
         x_pool = ctx.enter_context(tc.tile_pool(name="x_pool", bufs=X_BUFS))
+        sorted_pool = ctx.enter_context(tc.tile_pool(name="sorted_pool", bufs=2))
         grouped_pool = ctx.enter_context(tc.tile_pool(name="grouped_pool", bufs=2))
         quant_pool = ctx.enter_context(tc.tile_pool(name="quant_pool", bufs=3))
         res_pool = ctx.enter_context(tc.tile_pool(name="res_pool", bufs=2))
@@ -49,6 +49,7 @@ def tile_moelineara_e_kernel(tc, x, W_words, W_scales, *outs):
         ctx.enter_context(tc.manual_schedule())
 
         x_raw = {}
+        x_sorted = {}
         x_codes = {}
         x_planes = {}
         results = {}
@@ -57,18 +58,23 @@ def tile_moelineara_e_kernel(tc, x, W_words, W_scales, *outs):
             x_raw[j] = x_pool.tile([P, D], BF16, name="x_raw")
             nc.sync.dma_start(out=x_raw[j][:], in_=x_tiles[:, j, :])
 
+        def sort_tile(j):
+            x_sorted[j] = sorted_pool.tile([P, PASSES, 2, P], F32, name="x_sorted")
+            nc.vector.tensor_copy(
+                out=x_sorted[j][:],
+                in_=x_raw[j][:].bitcast(F32).rearrange("p (g w u) -> p g u w", g=PASSES, u=2),
+            )
+
         def transpose_tile(j):
-            words = x_raw[j][:].bitcast(F32)
             grouped = grouped_pool.tile([P, PASSES, P, PACK], BF16, name="grouped", align_bytes=64)
             grouped_words = grouped[:].bitcast(F32)
             for b in range(BANKS_TILE):
                 planes = psum_t.tile([P, PASSES_BANK, 2, P], F32, name="planes")
                 for a in range(PASSES_BANK):
-                    first = (b * PASSES_BANK + a) * WORDS_PASS
                     for u in range(2):
                         nc.tensor.transpose(
                             planes[:, a, u, :],
-                            words[:, first + u : first + WORDS_PASS : 2],
+                            x_sorted[j][:, b * PASSES_BANK + a, u, :],
                             identity[:],
                         )
                 nc.scalar.copy(
@@ -143,8 +149,11 @@ def tile_moelineara_e_kernel(tc, x, W_words, W_scales, *outs):
         for j in range(X_FIRST, X_BUFS):
             load_x(j)
 
-        grouped_next = transpose_tile(0)
+        sort_tile(0)
         load_x(X_BUFS)
+        sort_tile(1)
+        load_x(X_BUFS + 1)
+        grouped_next = transpose_tile(0)
         quantise_tile(0, grouped_next)
 
         w_planes = keep.tile([P, PASSES, N_ALL], U8, name="w_planes", align_bytes=64)
@@ -154,10 +163,12 @@ def tile_moelineara_e_kernel(tc, x, W_words, W_scales, *outs):
         )
 
         for j in range(TILES):
+            if j + 2 < TILES:
+                sort_tile(j + 2)
+            if j + 2 + X_BUFS < TILES:
+                load_x(j + 2 + X_BUFS)
             if j + 1 < TILES:
                 grouped_next = transpose_tile(j + 1)
-            if j + 1 + X_BUFS < TILES:
-                load_x(j + 1 + X_BUFS)
             acc = multiply_tile(j)
             if j + 1 < TILES:
                 quantise_tile(j + 1, grouped_next)

@@ -24,7 +24,8 @@ PASSES_BANK = 2
 BANKS_TILE = PASSES // PASSES_BANK
 PASSES_QUANT = 4
 X_BUFS = 8
-X_FIRST = 2
+HEAD = 4
+X_FIRST = HEAD + 2
 STORE_TILES = 4
 
 FLOPS = 2 * TOKENS * D * N_ALL
@@ -42,10 +43,10 @@ def tile_moelineara_e_kernel(tc, x, W_words, W_scales, *outs):
         x_pool = ctx.enter_context(tc.tile_pool(name="x_pool", bufs=X_BUFS))
         sorted_pool = ctx.enter_context(tc.tile_pool(name="sorted_pool", bufs=2))
         grouped_pool = ctx.enter_context(tc.tile_pool(name="grouped_pool", bufs=2))
-        quant_pool = ctx.enter_context(tc.tile_pool(name="quant_pool", bufs=3))
+        quant_pool = ctx.enter_context(tc.tile_pool(name="quant_pool", bufs=HEAD + 2))
         res_pool = ctx.enter_context(tc.tile_pool(name="res_pool", bufs=2))
         psum_t = ctx.enter_context(tc.psum_pool(name="psum_t", bufs=BANKS_TILE))
-        psum_acc = ctx.enter_context(tc.psum_pool(name="psum_acc", bufs=4))
+        psum_acc = ctx.enter_context(tc.psum_pool(name="psum_acc", bufs=HEAD))
         ctx.enter_context(tc.manual_schedule())
 
         x_raw = {}
@@ -94,33 +95,37 @@ def tile_moelineara_e_kernel(tc, x, W_words, W_scales, *outs):
                     in_=grouped[:, some, :, :].rearrange("p g r t -> p (g r t)"),
                 )
 
-        def multiply_tile(j):
-            acc = psum_acc.tile([P, N_ALL], F32, name="acc")
+        def multiply_tiles(tiles):
+            sums = {}
+            for j in tiles:
+                sums[j] = psum_acc.tile([P, N_ALL], F32, name="sums")
             for g in range(PASSES):
-                nc.tensor.matmul_mx(
-                    out=acc[:],
-                    lhsT=x_codes[j][:, g, :].bitcast(FP8X4),
-                    lhsT_scale=x_planes[j][:, g, :],
-                    rhs=w_codes[:, g, :].bitcast(FP8X4),
-                    rhs_scale=w_planes[:, g, :],
-                    start=(g == 0),
-                    stop=(g == PASSES - 1),
-                )
-            return acc
+                for j in tiles:
+                    nc.tensor.matmul_mx(
+                        out=sums[j][:],
+                        lhsT=x_codes[j][:, g, :].bitcast(FP8X4),
+                        lhsT_scale=x_planes[j][:, g, :],
+                        rhs=w_codes[:, g, :].bitcast(FP8X4),
+                        rhs_scale=w_planes[:, g, :],
+                        start=(g == 0),
+                        stop=(g == PASSES - 1),
+                    )
+            return sums
 
         def store_tile(j, acc):
             group, i = divmod(j, STORE_TILES)
             if i == 0:
                 results[group] = res_pool.tile([P, EXPERTS, STORE_TILES, RANK], F32, name="results")
-            nc.vector.tensor_copy(
+            nc.scalar.copy(
                 out=results[group][:, :, i, :],
                 in_=acc[:].rearrange("p (e r) -> p e r", e=EXPERTS),
             )
-            if i == STORE_TILES - 1:
+            if i == STORE_TILES - 1 or j == TILES - 2:
+                first = i if j == TILES - 1 else 0
                 for e in range(EXPERTS):
                     nc.sync.dma_start(
-                        out=out_tiles[e][:, group * STORE_TILES : (group + 1) * STORE_TILES, :],
-                        in_=results[group][:, e, :, :],
+                        out=out_tiles[e][:, group * STORE_TILES + first : j + 1, :],
+                        in_=results[group][:, e, first : i + 1, :],
                     )
 
         identity = keep.tile([P, P], F32, name="identity")
@@ -129,12 +134,17 @@ def tile_moelineara_e_kernel(tc, x, W_words, W_scales, *outs):
         w_planes_by_group = keep.tile([P, EXPERTS * PASSES, RANK], U8, name="w_planes_by_group")
         nc.vector.memset(w_planes_by_group[:].bitcast(I32), 0)
         for quadrant in range(4):
-            nc.gpsimd.dma_start(
-                out=w_planes_by_group[32 * quadrant : 32 * quadrant + 4, :, :].bitcast(F32),
+            nc.sync.dma_start(
+                out=w_planes_by_group[32 * quadrant : 32 * quadrant + 4, :, :].bitcast(I32),
                 in_=W_scales[:, 4 * quadrant : 4 * quadrant + 4, :]
                 .rearrange("c r n -> r c n")
-                .bitcast(F32),
+                .bitcast(I32),
             )
+        w_planes = keep.tile([P, PASSES, N_ALL], U8, name="w_planes", align_bytes=64)
+        nc.vector.tensor_copy(
+            out=w_planes[:].bitcast(I32).rearrange("p g (e n) -> p g e n", e=EXPERTS),
+            in_=w_planes_by_group[:].bitcast(I32).rearrange("p (e g) n -> p g e n", g=PASSES),
+        )
 
         for j in range(X_FIRST):
             load_x(j)
@@ -156,12 +166,7 @@ def tile_moelineara_e_kernel(tc, x, W_words, W_scales, *outs):
         grouped_next = transpose_tile(0)
         quantise_tile(0, grouped_next)
 
-        w_planes = keep.tile([P, PASSES, N_ALL], U8, name="w_planes", align_bytes=64)
-        nc.vector.tensor_copy(
-            out=w_planes[:].bitcast(I32).rearrange("p g (e n) -> p g e n", e=EXPERTS),
-            in_=w_planes_by_group[:].bitcast(I32).rearrange("p (e g) n -> p g e n", g=PASSES),
-        )
-
+        waiting = []
         for j in range(TILES):
             if j + 2 < TILES:
                 sort_tile(j + 2)
@@ -169,7 +174,12 @@ def tile_moelineara_e_kernel(tc, x, W_words, W_scales, *outs):
                 load_x(j + 2 + X_BUFS)
             if j + 1 < TILES:
                 grouped_next = transpose_tile(j + 1)
-            acc = multiply_tile(j)
+            waiting.append(j)
+            if j + 1 >= HEAD:
+                sums = multiply_tiles(waiting)
             if j + 1 < TILES:
                 quantise_tile(j + 1, grouped_next)
-            store_tile(j, acc)
+            if j + 1 >= HEAD:
+                for i in waiting:
+                    store_tile(i, sums[i])
+                waiting = []

@@ -22,9 +22,11 @@ PASSES = D // K_PASS
 TILES = TOKENS // P
 PASSES_BANK = 2
 BANKS_TILE = PASSES // PASSES_BANK
+PSUM_BANKS = 8
 PASSES_QUANT = 4
 X_BUFS = 8
 HEAD = 4
+ROUND = 2
 X_FIRST = HEAD + 2
 STORE_TILES = 4
 
@@ -45,14 +47,14 @@ def tile_moelineara_e_kernel(tc, x, W_words, W_scales, *outs):
         grouped_pool = ctx.enter_context(tc.tile_pool(name="grouped_pool", bufs=2))
         quant_pool = ctx.enter_context(tc.tile_pool(name="quant_pool", bufs=HEAD + 2))
         res_pool = ctx.enter_context(tc.tile_pool(name="res_pool", bufs=2))
-        psum_t = ctx.enter_context(tc.psum_pool(name="psum_t", bufs=BANKS_TILE))
-        psum_acc = ctx.enter_context(tc.psum_pool(name="psum_acc", bufs=HEAD))
+        psum = ctx.enter_context(tc.psum_pool(name="psum", bufs=PSUM_BANKS))
         ctx.enter_context(tc.manual_schedule())
 
         x_raw = {}
         x_sorted = {}
         x_codes = {}
         x_planes = {}
+        sums = {}
         results = {}
 
         def load_x(j):
@@ -70,7 +72,7 @@ def tile_moelineara_e_kernel(tc, x, W_words, W_scales, *outs):
             grouped = grouped_pool.tile([P, PASSES, P, PACK], BF16, name="grouped", align_bytes=64)
             grouped_words = grouped[:].bitcast(F32)
             for b in range(BANKS_TILE):
-                planes = psum_t.tile([P, PASSES_BANK, 2, P], F32, name="planes")
+                planes = psum.tile([P, PASSES_BANK, 2, P], F32, name="planes", tag="bank")
                 for a in range(PASSES_BANK):
                     for u in range(2):
                         nc.tensor.transpose(
@@ -96,9 +98,8 @@ def tile_moelineara_e_kernel(tc, x, W_words, W_scales, *outs):
                 )
 
         def multiply_tiles(tiles):
-            sums = {}
             for j in tiles:
-                sums[j] = psum_acc.tile([P, N_ALL], F32, name="sums")
+                sums[j] = psum.tile([P, N_ALL], F32, name="sums", tag="bank")
             for g in range(PASSES):
                 for j in tiles:
                     nc.tensor.matmul_mx(
@@ -110,15 +111,14 @@ def tile_moelineara_e_kernel(tc, x, W_words, W_scales, *outs):
                         start=(g == 0),
                         stop=(g == PASSES - 1),
                     )
-            return sums
 
-        def store_tile(j, acc):
+        def store_tile(j):
             group, i = divmod(j, STORE_TILES)
             if i == 0:
                 results[group] = res_pool.tile([P, EXPERTS, STORE_TILES, RANK], F32, name="results")
             nc.scalar.copy(
                 out=results[group][:, :, i, :],
-                in_=acc[:].rearrange("p (e r) -> p e r", e=EXPERTS),
+                in_=sums[j][:].rearrange("p (e r) -> p e r", e=EXPERTS),
             )
             if i == STORE_TILES - 1 or j == TILES - 2:
                 first = i if j == TILES - 1 else 0
@@ -174,12 +174,14 @@ def tile_moelineara_e_kernel(tc, x, W_words, W_scales, *outs):
                 load_x(j + 2 + X_BUFS)
             if j + 1 < TILES:
                 grouped_next = transpose_tile(j + 1)
-            waiting.append(j)
-            if j + 1 >= HEAD:
-                sums = multiply_tiles(waiting)
-            if j + 1 < TILES:
                 quantise_tile(j + 1, grouped_next)
-            if j + 1 >= HEAD:
+            waiting.append(j)
+            if j == HEAD - 1:
+                multiply_tiles(waiting)
+            if j >= HEAD and len(waiting) == ROUND:
                 for i in waiting:
-                    store_tile(i, sums[i])
+                    multiply_tiles([i])
+            if j == HEAD - 1 or (j >= HEAD and len(waiting) == ROUND):
+                for i in waiting:
+                    store_tile(i)
                 waiting = []

@@ -43,10 +43,10 @@ def tile_moelineara_e_kernel(tc, x, W_words, W_scales, *outs):
     with ExitStack() as ctx:
         keep = ctx.enter_context(tc.tile_pool(name="keep", bufs=1))
         x_pool = ctx.enter_context(tc.tile_pool(name="x_pool", bufs=X_BUFS))
-        sorted_pool = ctx.enter_context(tc.tile_pool(name="sorted_pool", bufs=2))
+        sorted_pool = ctx.enter_context(tc.tile_pool(name="sorted_pool", bufs=4))
         grouped_pool = ctx.enter_context(tc.tile_pool(name="grouped_pool", bufs=2))
         quant_pool = ctx.enter_context(tc.tile_pool(name="quant_pool", bufs=HEAD + 2))
-        res_pool = ctx.enter_context(tc.tile_pool(name="res_pool", bufs=2))
+        res_pool = ctx.enter_context(tc.tile_pool(name="res_pool", bufs=TILES // STORE_TILES))
         psum = ctx.enter_context(tc.psum_pool(name="psum", bufs=PSUM_BANKS))
         ctx.enter_context(tc.manual_schedule())
 
@@ -57,16 +57,25 @@ def tile_moelineara_e_kernel(tc, x, W_words, W_scales, *outs):
         sums = {}
         results = {}
 
+        def pieces(j):
+            return 4 if j < X_BUFS else 1
+
         def load_x(j):
             x_raw[j] = x_pool.tile([P, D], BF16, name="x_raw")
-            nc.sync.dma_start(out=x_raw[j][:], in_=x_tiles[:, j, :])
+            width = D // pieces(j)
+            for c in range(pieces(j)):
+                cols = slice(c * width, (c + 1) * width)
+                nc.sync.dma_start(out=x_raw[j][:, cols], in_=x_tiles[:, j, cols])
 
         def sort_tile(j):
             x_sorted[j] = sorted_pool.tile([P, PASSES, 2, P], F32, name="x_sorted")
-            nc.vector.tensor_copy(
-                out=x_sorted[j][:],
-                in_=x_raw[j][:].bitcast(F32).rearrange("p (g w u) -> p g u w", g=PASSES, u=2),
-            )
+            words = x_raw[j][:].bitcast(F32).rearrange("p (g w u) -> p g u w", g=PASSES, u=2)
+            some = PASSES // pieces(j)
+            for c in range(pieces(j)):
+                nc.vector.tensor_copy(
+                    out=x_sorted[j][:, c * some : (c + 1) * some, :, :],
+                    in_=words[:, c * some : (c + 1) * some, :, :],
+                )
 
         def transpose_tile(j):
             grouped = grouped_pool.tile([P, PASSES, P, PACK], BF16, name="grouped", align_bytes=64)
@@ -131,8 +140,12 @@ def tile_moelineara_e_kernel(tc, x, W_words, W_scales, *outs):
         identity = keep.tile([P, P], F32, name="identity")
         make_identity(nc, identity[:])
 
+        load_x(0)
+
         w_planes_by_group = keep.tile([P, EXPERTS * PASSES, RANK], U8, name="w_planes_by_group")
         nc.vector.memset(w_planes_by_group[:].bitcast(I32), 0)
+        for j in range(1, HEAD):
+            load_x(j)
         for quadrant in range(4):
             nc.sync.dma_start(
                 out=w_planes_by_group[32 * quadrant : 32 * quadrant + 4, :, :].bitcast(I32),
@@ -141,13 +154,6 @@ def tile_moelineara_e_kernel(tc, x, W_words, W_scales, *outs):
                 .bitcast(I32),
             )
         w_planes = keep.tile([P, PASSES, N_ALL], U8, name="w_planes", align_bytes=64)
-        nc.vector.tensor_copy(
-            out=w_planes[:].bitcast(I32).rearrange("p g (e n) -> p g e n", e=EXPERTS),
-            in_=w_planes_by_group[:].bitcast(I32).rearrange("p (e g) n -> p g e n", g=PASSES),
-        )
-
-        for j in range(X_FIRST):
-            load_x(j)
 
         w_codes = keep.tile([P, PASSES, N_ALL], U32, name="w_codes", align_bytes=64)
         for g in range(PASSES):
@@ -156,32 +162,43 @@ def tile_moelineara_e_kernel(tc, x, W_words, W_scales, *outs):
                 in_=w_words_by_pass[g].bitcast(I32),
             )
 
-        for j in range(X_FIRST, X_BUFS):
+        for j in range(HEAD, X_BUFS):
             load_x(j)
 
-        sort_tile(0)
-        load_x(X_BUFS)
-        sort_tile(1)
-        load_x(X_BUFS + 1)
-        grouped_next = transpose_tile(0)
-        quantise_tile(0, grouped_next)
+        def sort_ahead(j):
+            if j < TILES:
+                sort_tile(j)
+            if j + X_BUFS < TILES:
+                load_x(j + X_BUFS)
 
-        waiting = []
-        for j in range(TILES):
-            if j + 2 < TILES:
-                sort_tile(j + 2)
-            if j + 2 + X_BUFS < TILES:
-                load_x(j + 2 + X_BUFS)
-            if j + 1 < TILES:
-                grouped_next = transpose_tile(j + 1)
-                quantise_tile(j + 1, grouped_next)
-            waiting.append(j)
+        def prepare(j):
+            quantise_tile(j, transpose_tile(j))
+
+        sort_ahead(0)
+        sort_ahead(1)
+        for j in range(HEAD):
             if j == HEAD - 1:
-                multiply_tiles(waiting)
-            if j >= HEAD and len(waiting) == ROUND:
-                for i in waiting:
-                    multiply_tiles([i])
-            if j == HEAD - 1 or (j >= HEAD and len(waiting) == ROUND):
-                for i in waiting:
-                    store_tile(i)
-                waiting = []
+                nc.vector.tensor_copy(
+                    out=w_planes[:].bitcast(I32).rearrange("p g (e n) -> p g e n", e=EXPERTS),
+                    in_=w_planes_by_group[:].bitcast(I32).rearrange("p (e g) n -> p g e n", g=PASSES),
+                )
+            prepare(j)
+            if j + 2 < HEAD:
+                sort_ahead(j + 2)
+        sort_ahead(HEAD)
+        sort_ahead(HEAD + 1)
+        multiply_tiles(list(range(HEAD)))
+        for i in range(HEAD):
+            store_tile(i)
+
+        multiplied = HEAD
+        for first in range(HEAD, TILES, ROUND):
+            for j in range(first, first + ROUND):
+                prepare(j)
+                sort_ahead(j + 2)
+            last = TILES if first + ROUND == TILES else first + 1
+            for i in range(multiplied, last):
+                multiply_tiles([i])
+            for i in range(multiplied, last):
+                store_tile(i)
+            multiplied = last

@@ -12,23 +12,24 @@ U8 = mybir.dt.uint8
 
 P = 128
 PACK = 4
-K_PASS = P * PACK
 TOKENS = 2 * 1024
 D = 4096
 EXPERTS = 8
 RANK = 64
 N_ALL = EXPERTS * RANK
-PASSES = D // K_PASS
+PASSES = D // (P * PACK)
 TILES = TOKENS // P
+QUADS = 4
+LANES = P // QUADS
+D_QUAD = D // QUADS
 PASSES_BANK = 2
 BANKS_TILE = PASSES // PASSES_BANK
 PSUM_BANKS = 8
-PASSES_QUANT = 4
+HALF = PASSES // 2
 X_BUFS = 8
 HEAD = 4
-ROUND = 2
-X_FIRST = HEAD + 2
 STORE_TILES = 4
+ON_VECTOR = (6, 9, 12, 15)
 
 FLOPS = 2 * TOKENS * D * N_ALL
 
@@ -36,15 +37,19 @@ FLOPS = 2 * TOKENS * D * N_ALL
 def tile_moelineara_e_kernel(tc, x, W_words, W_scales, *outs):
     nc = tc.nc
 
-    x_tiles = x.flatten_outer_dims().rearrange("(p j) k -> p j k", j=TILES)
+    x_rows = x.flatten_outer_dims()
+    x_tiles = x_rows.rearrange("(m j) k -> m j k", j=TILES)
+    x_lanes = x_rows.rearrange("(a b j) k -> j b a k", a=QUADS, b=LANES)
     out_tiles = [o.flatten_outer_dims().rearrange("(p j) r -> p j r", j=TILES) for o in outs]
-    w_words_by_pass = W_words.rearrange("(e g) p n t -> g p e (n t)", g=PASSES)
+    w_words_by_group = W_words.rearrange("(e c) p n t -> c p e (n t)", c=PASSES)
+    w_scales_by_group = W_scales.rearrange("(e c) q n -> c q e n", c=PASSES)
 
     with ExitStack() as ctx:
         keep = ctx.enter_context(tc.tile_pool(name="keep", bufs=1))
         x_pool = ctx.enter_context(tc.tile_pool(name="x_pool", bufs=X_BUFS))
         sorted_pool = ctx.enter_context(tc.tile_pool(name="sorted_pool", bufs=4))
-        grouped_pool = ctx.enter_context(tc.tile_pool(name="grouped_pool", bufs=2))
+        turned_pool = ctx.enter_context(tc.tile_pool(name="turned_pool", bufs=1))
+        grouped_pool = ctx.enter_context(tc.tile_pool(name="grouped_pool", bufs=3))
         quant_pool = ctx.enter_context(tc.tile_pool(name="quant_pool", bufs=HEAD + 2))
         res_pool = ctx.enter_context(tc.tile_pool(name="res_pool", bufs=TILES // STORE_TILES))
         psum = ctx.enter_context(tc.psum_pool(name="psum", bufs=PSUM_BANKS))
@@ -52,34 +57,45 @@ def tile_moelineara_e_kernel(tc, x, W_words, W_scales, *outs):
 
         x_raw = {}
         x_sorted = {}
+        x_turned = {}
+        x_grouped = {}
         x_codes = {}
         x_planes = {}
         sums = {}
         results = {}
 
-        def pieces(j):
-            return 4 if j < X_BUFS else 1
-
         def load_x(j):
             x_raw[j] = x_pool.tile([P, D], BF16, name="x_raw")
-            width = D // pieces(j)
-            for c in range(pieces(j)):
-                cols = slice(c * width, (c + 1) * width)
-                nc.sync.dma_start(out=x_raw[j][:, cols], in_=x_tiles[:, j, cols])
+            if j in ON_VECTOR:
+                for q in range(QUADS):
+                    nc.sync.dma_start(
+                        out=x_raw[j][q * LANES : (q + 1) * LANES, :].rearrange("b (a k) -> b a k", a=QUADS),
+                        in_=x_lanes[j][:, :, q * D_QUAD : (q + 1) * D_QUAD],
+                    )
+            else:
+                nc.sync.dma_start(out=x_raw[j][:], in_=x_tiles[:, j, :])
 
         def sort_tile(j):
-            x_sorted[j] = sorted_pool.tile([P, PASSES, 2, P], F32, name="x_sorted")
-            words = x_raw[j][:].bitcast(F32).rearrange("p (g w u) -> p g u w", g=PASSES, u=2)
-            some = PASSES // pieces(j)
-            for c in range(pieces(j)):
+            x_sorted[j] = sorted_pool.tile([P, PASSES, 2, P], F32, name="x_sorted", align_bytes=64)
+            words = x_raw[j][:].bitcast(F32).rearrange("p (s g i u) -> p u g s i", s=QUADS, g=PASSES, u=2)
+            for u in range(2):
                 nc.vector.tensor_copy(
-                    out=x_sorted[j][:, c * some : (c + 1) * some, :, :],
-                    in_=words[:, c * some : (c + 1) * some, :, :],
+                    out=x_sorted[j][:, :, u, :].rearrange("p g (s i) -> p g s i", s=QUADS),
+                    in_=words[:, u],
                 )
 
+        def sort_ahead(j):
+            if j < TILES:
+                sort_tile(j)
+            if j + X_BUFS < TILES:
+                load_x(j + X_BUFS)
+
+        def new_grouped(j):
+            x_grouped[j] = grouped_pool.tile([P, PASSES, P, PACK], BF16, name="grouped", align_bytes=64)
+            return x_grouped[j][:].bitcast(F32)
+
         def transpose_tile(j):
-            grouped = grouped_pool.tile([P, PASSES, P, PACK], BF16, name="grouped", align_bytes=64)
-            grouped_words = grouped[:].bitcast(F32)
+            grouped_words = new_grouped(j)
             for b in range(BANKS_TILE):
                 planes = psum.tile([P, PASSES_BANK, 2, P], F32, name="planes", tag="bank")
                 for a in range(PASSES_BANK):
@@ -93,18 +109,37 @@ def tile_moelineara_e_kernel(tc, x, W_words, W_scales, *outs):
                     out=grouped_words[:, b * PASSES_BANK : (b + 1) * PASSES_BANK, :, :],
                     in_=planes[:].rearrange("p a u r -> p a r u"),
                 )
-            return grouped
 
-        def quantise_tile(j, grouped):
-            x_codes[j] = quant_pool.tile([P, PASSES, P], U32, name="x_codes", align_bytes=64)
-            x_planes[j] = quant_pool.tile([P, PASSES, P], U8, name="x_planes", align_bytes=64)
-            for g in range(0, PASSES, PASSES_QUANT):
-                some = slice(g, g + PASSES_QUANT)
-                nc.vector.quantize_mx(
-                    out=x_codes[j][:, some, :].rearrange("p g r -> p (g r)").bitcast(FP8X4),
-                    scales=x_planes[j][:, some, :].rearrange("p g r -> p (g r)"),
-                    in_=grouped[:, some, :, :].rearrange("p g r t -> p (g r t)"),
+        def turn_tile(j):
+            x_turned[j] = turned_pool.tile([P, PASSES, 2, P], F32, name="turned", align_bytes=64)
+            nc.vector.transpose(
+                x_turned[j][:].rearrange("p g u r -> p (g u r)"),
+                x_sorted[j][:].rearrange("p g u r -> p (g u r)"),
+            )
+
+        def interleave_tile(j):
+            grouped_words = new_grouped(j)
+            for h in range(2):
+                some = slice(h * HALF, (h + 1) * HALF)
+                nc.scalar.copy(
+                    out=grouped_words[:, some, :, :],
+                    in_=x_turned[j][:, some, :, :].rearrange("p g u r -> p g r u"),
                 )
+
+        def quantise_half(j, h):
+            if h == 0:
+                x_codes[j] = quant_pool.tile([P, PASSES, P], U32, name="x_codes", align_bytes=64)
+                x_planes[j] = quant_pool.tile([P, PASSES, P], U8, name="x_planes", align_bytes=64)
+            some = slice(h * HALF, (h + 1) * HALF)
+            nc.vector.quantize_mx(
+                out=x_codes[j][:, some, :].rearrange("p g r -> p (g r)").bitcast(FP8X4),
+                scales=x_planes[j][:, some, :].rearrange("p g r -> p (g r)"),
+                in_=x_grouped[j][:, some, :, :].rearrange("p g r t -> p (g r t)"),
+            )
+
+        def quantise_tile(j):
+            quantise_half(j, 0)
+            quantise_half(j, 1)
 
         def multiply_tiles(tiles):
             for j in tiles:
@@ -116,7 +151,7 @@ def tile_moelineara_e_kernel(tc, x, W_words, W_scales, *outs):
                         lhsT=x_codes[j][:, g, :].bitcast(FP8X4),
                         lhsT_scale=x_planes[j][:, g, :],
                         rhs=w_codes[:, g, :].bitcast(FP8X4),
-                        rhs_scale=w_planes[:, g, :],
+                        rhs_scale=w_planes[PACK * (g % HALF) : P, g // HALF, :],
                         start=(g == 0),
                         stop=(g == PASSES - 1),
                     )
@@ -137,68 +172,78 @@ def tile_moelineara_e_kernel(tc, x, W_words, W_scales, *outs):
                         in_=results[group][:, e, first : i + 1, :],
                     )
 
+        def multiply_and_store(tiles):
+            for i in tiles:
+                multiply_tiles([i])
+            for i in tiles:
+                store_tile(i)
+
         identity = keep.tile([P, P], F32, name="identity")
         make_identity(nc, identity[:])
 
-        load_x(0)
-
-        w_planes_by_group = keep.tile([P, EXPERTS * PASSES, RANK], U8, name="w_planes_by_group")
-        nc.vector.memset(w_planes_by_group[:].bitcast(I32), 0)
-        for j in range(1, HEAD):
+        for j in range(HEAD):
             load_x(j)
-        for quadrant in range(4):
-            nc.sync.dma_start(
-                out=w_planes_by_group[32 * quadrant : 32 * quadrant + 4, :, :].bitcast(I32),
-                in_=W_scales[:, 4 * quadrant : 4 * quadrant + 4, :]
-                .rearrange("c r n -> r c n")
-                .bitcast(I32),
-            )
-        w_planes = keep.tile([P, PASSES, N_ALL], U8, name="w_planes", align_bytes=64)
 
+        w_planes = keep.tile([P, 2, N_ALL], U8, name="w_planes", align_bytes=64)
+        nc.vector.memset(w_planes[:].bitcast(I32), 0)
+        for q in range(QUADS):
+            for c in range(2):
+                nc.sync.dma_start(
+                    out=w_planes[q * LANES : q * LANES + 16, c, :].bitcast(I32).rearrange("q (e n) -> q e n", e=EXPERTS),
+                    in_=w_scales_by_group[2 * q + c].bitcast(I32),
+                )
         w_codes = keep.tile([P, PASSES, N_ALL], U32, name="w_codes", align_bytes=64)
         for g in range(PASSES):
-            nc.sync.dma_start(
-                out=w_codes[:, g, :].bitcast(I32).rearrange("p (e n) -> p e n", e=EXPERTS),
-                in_=w_words_by_pass[g].bitcast(I32),
-            )
+            for q in range(QUADS):
+                first = LANES * (g % HALF)
+                nc.sync.dma_start(
+                    out=w_codes[q * LANES : (q + 1) * LANES, g, :].bitcast(I32).rearrange("p (e n) -> p e n", e=EXPERTS),
+                    in_=w_words_by_group[2 * q + g // HALF][first : first + LANES].bitcast(I32),
+                )
 
         for j in range(HEAD, X_BUFS):
             load_x(j)
 
-        def sort_ahead(j):
-            if j < TILES:
-                sort_tile(j)
-            if j + X_BUFS < TILES:
-                load_x(j + X_BUFS)
-
-        def prepare(j):
-            quantise_tile(j, transpose_tile(j))
-
         sort_ahead(0)
         sort_ahead(1)
         for j in range(HEAD):
-            if j == HEAD - 1:
-                nc.vector.tensor_copy(
-                    out=w_planes[:].bitcast(I32).rearrange("p g (e n) -> p g e n", e=EXPERTS),
-                    in_=w_planes_by_group[:].bitcast(I32).rearrange("p (e g) n -> p g e n", g=PASSES),
-                )
-            prepare(j)
+            transpose_tile(j)
+            quantise_tile(j)
             if j + 2 < HEAD:
                 sort_ahead(j + 2)
-        sort_ahead(HEAD)
-        sort_ahead(HEAD + 1)
+        sort_ahead(4)
+        sort_ahead(5)
         multiply_tiles(list(range(HEAD)))
         for i in range(HEAD):
             store_tile(i)
 
-        multiplied = HEAD
-        for first in range(HEAD, TILES, ROUND):
-            for j in range(first, first + ROUND):
-                prepare(j)
-                sort_ahead(j + 2)
-            last = TILES if first + ROUND == TILES else first + 1
-            for i in range(multiplied, last):
-                multiply_tiles([i])
-            for i in range(multiplied, last):
-                store_tile(i)
-            multiplied = last
+        transpose_tile(4)
+        quantise_tile(4)
+        sort_ahead(6)
+        transpose_tile(5)
+        quantise_tile(5)
+        sort_ahead(7)
+        turn_tile(6)
+        sort_ahead(8)
+        multiply_tiles([4])
+        multiply_tiles([5])
+        store_tile(4)
+        interleave_tile(6)
+        store_tile(5)
+        quantise_tile(6)
+        sort_ahead(9)
+
+        for c in ON_VECTOR[:-1]:
+            a, b, coming = c + 1, c + 2, c + 3
+            transpose_tile(a)
+            quantise_half(a, 0)
+            turn_tile(coming)
+            quantise_half(a, 1)
+            transpose_tile(b)
+            quantise_tile(b)
+            interleave_tile(coming)
+            sort_ahead(a + 3)
+            sort_ahead(b + 3)
+            quantise_tile(coming)
+            sort_ahead(coming + 3)
+            multiply_and_store([c, a, b] + ([coming] if coming == TILES - 1 else []))

@@ -67,22 +67,37 @@ def tile_moelineara_e_kernel(tc, x, W_words, W_scales, *outs):
         def load_x(j):
             x_raw[j] = x_pool.tile([P, D], BF16, name="x_raw")
             if j in ON_VECTOR:
+                load_quadrants(j, nc.sync, (0, 1))
+            elif j < X_BUFS:
                 for q in range(QUADS):
-                    nc.sync.dma_start(
-                        out=x_raw[j][q * LANES : (q + 1) * LANES, :].rearrange("b (a k) -> b a k", a=QUADS),
-                        in_=x_lanes[j][:, :, q * D_QUAD : (q + 1) * D_QUAD],
-                    )
+                    cols = slice(q * D_QUAD, (q + 1) * D_QUAD)
+                    nc.sync.dma_start(out=x_raw[j][:, cols], in_=x_tiles[:, j, cols])
             else:
                 nc.sync.dma_start(out=x_raw[j][:], in_=x_tiles[:, j, :])
 
+        def load_quadrants(j, queue, quadrants):
+            for q in quadrants:
+                queue.dma_start(
+                    out=x_raw[j][q * LANES : (q + 1) * LANES, :].rearrange("b (a k) -> b a k", a=QUADS),
+                    in_=x_lanes[j][:, :, q * D_QUAD : (q + 1) * D_QUAD],
+                )
+
         def sort_tile(j):
             x_sorted[j] = sorted_pool.tile([P, PASSES, 2, P], F32, name="x_sorted", align_bytes=64)
-            words = x_raw[j][:].bitcast(F32).rearrange("p (s g i u) -> p u g s i", s=QUADS, g=PASSES, u=2)
-            for u in range(2):
-                nc.vector.tensor_copy(
-                    out=x_sorted[j][:, :, u, :].rearrange("p g (s i) -> p g s i", s=QUADS),
-                    in_=words[:, u],
-                )
+            if j < X_BUFS and j not in ON_VECTOR:
+                words = x_raw[j][:].bitcast(F32).rearrange("p (s g i u) -> p s g u i", s=QUADS, g=PASSES, u=2)
+                for s in range(QUADS):
+                    nc.vector.tensor_copy(
+                        out=x_sorted[j][:, :, :, s * LANES : (s + 1) * LANES],
+                        in_=words[:, s],
+                    )
+            else:
+                words = x_raw[j][:].bitcast(F32).rearrange("p (s g i u) -> p u g s i", s=QUADS, g=PASSES, u=2)
+                for u in range(2):
+                    nc.vector.tensor_copy(
+                        out=x_sorted[j][:, :, u, :].rearrange("p g (s i) -> p g s i", s=QUADS),
+                        in_=words[:, u],
+                    )
 
         def sort_ahead(j):
             if j < TILES:
@@ -156,11 +171,12 @@ def tile_moelineara_e_kernel(tc, x, W_words, W_scales, *outs):
                         stop=(g == PASSES - 1),
                     )
 
-        def store_tile(j):
+        def store_tile(j, on_vector=False):
             group, i = divmod(j, STORE_TILES)
             if i == 0:
                 results[group] = res_pool.tile([P, EXPERTS, STORE_TILES, RANK], F32, name="results")
-            nc.scalar.copy(
+            copy = nc.vector.tensor_copy if on_vector else nc.scalar.copy
+            copy(
                 out=results[group][:, :, i, :],
                 in_=sums[j][:].rearrange("p (e r) -> p e r", e=EXPERTS),
             )
@@ -194,7 +210,7 @@ def tile_moelineara_e_kernel(tc, x, W_words, W_scales, *outs):
                 )
         w_codes = keep.tile([P, PASSES, N_ALL], U32, name="w_codes", align_bytes=64)
         for g in range(PASSES):
-            for q in range(QUADS):
+            for q in (0, 2, 1, 3):
                 first = LANES * (g % HALF)
                 nc.sync.dma_start(
                     out=w_codes[q * LANES : (q + 1) * LANES, g, :].bitcast(I32).rearrange("p (e n) -> p e n", e=EXPERTS),
@@ -212,15 +228,19 @@ def tile_moelineara_e_kernel(tc, x, W_words, W_scales, *outs):
             if j + 2 < HEAD:
                 sort_ahead(j + 2)
         sort_ahead(4)
-        sort_ahead(5)
         multiply_tiles(list(range(HEAD)))
-        for i in range(HEAD):
-            store_tile(i)
+        store_tile(0)
+        load_quadrants(6, nc.scalar, (2, 3))
+        store_tile(1)
+        store_tile(2, on_vector=True)
+        store_tile(3, on_vector=True)
+        sort_ahead(5)
 
         transpose_tile(4)
         quantise_tile(4)
         sort_ahead(6)
         transpose_tile(5)
+        load_quadrants(9, nc.scalar, (2, 3))
         quantise_tile(5)
         sort_ahead(7)
         turn_tile(6)
@@ -236,10 +256,14 @@ def tile_moelineara_e_kernel(tc, x, W_words, W_scales, *outs):
         for c in ON_VECTOR[:-1]:
             a, b, coming = c + 1, c + 2, c + 3
             transpose_tile(a)
+            if c == ON_VECTOR[0]:
+                load_quadrants(12, nc.scalar, (2, 3))
             quantise_half(a, 0)
             turn_tile(coming)
             quantise_half(a, 1)
             transpose_tile(b)
+            if c == ON_VECTOR[0]:
+                load_quadrants(15, nc.scalar, (2, 3))
             quantise_tile(b)
             interleave_tile(coming)
             sort_ahead(a + 3)

@@ -29,7 +29,7 @@ HALF = PASSES // 2
 X_BUFS = 8
 HEAD = 4
 STORE_TILES = 4
-ON_VECTOR = (6, 9, 12, 15)
+ON_VECTOR = ()
 
 FLOPS = 2 * TOKENS * D * N_ALL
 
@@ -228,46 +228,17 @@ def tile_moelineara_e_kernel(tc, x, W_words, W_scales, *outs):
             if j + 2 < HEAD:
                 sort_ahead(j + 2)
         sort_ahead(4)
-        multiply_tiles(list(range(HEAD)))
-        store_tile(0)
-        load_quadrants(6, nc.scalar, (2, 3))
-        store_tile(1)
-        store_tile(2, on_vector=True)
-        store_tile(3, on_vector=True)
         sort_ahead(5)
+        multiply_tiles(list(range(HEAD)))
+        for i in range(HEAD):
+            store_tile(i)
 
-        transpose_tile(4)
-        quantise_tile(4)
-        sort_ahead(6)
-        transpose_tile(5)
-        load_quadrants(9, nc.scalar, (2, 3))
-        quantise_tile(5)
-        sort_ahead(7)
-        turn_tile(6)
-        sort_ahead(8)
-        multiply_tiles([4])
-        multiply_tiles([5])
-        store_tile(4)
-        interleave_tile(6)
-        store_tile(5)
-        quantise_tile(6)
-        sort_ahead(9)
-
-        for c in ON_VECTOR[:-1]:
-            a, b, coming = c + 1, c + 2, c + 3
-            transpose_tile(a)
-            if c == ON_VECTOR[0]:
-                load_quadrants(12, nc.scalar, (2, 3))
-            quantise_half(a, 0)
-            turn_tile(coming)
-            quantise_half(a, 1)
-            transpose_tile(b)
-            if c == ON_VECTOR[0]:
-                load_quadrants(15, nc.scalar, (2, 3))
-            quantise_tile(b)
-            interleave_tile(coming)
-            sort_ahead(a + 3)
-            sort_ahead(b + 3)
-            quantise_tile(coming)
-            sort_ahead(coming + 3)
-            multiply_and_store([c, a, b] + ([coming] if coming == TILES - 1 else []))
+        multiplied = HEAD
+        for first in range(HEAD, TILES, 2):
+            for j in range(first, first + 2):
+                transpose_tile(j)
+                quantise_tile(j)
+                sort_ahead(j + 2)
+            last = TILES if first + 2 == TILES else first + 1
+            multiply_and_store(list(range(multiplied, last)))
+            multiplied = last

@@ -224,9 +224,9 @@ def tile_moelineara_e_kernel(tc, x, W_words, W_scales, *outs):
         sort_ahead(1)
         for j in range(HEAD):
             transpose_tile(j)
-            quantise_tile(j)
             if j + 2 < HEAD:
                 sort_ahead(j + 2)
+            quantise_tile(j)
         sort_ahead(4)
         sort_ahead(5)
         multiply_tiles(list(range(HEAD)))

from contextlib import ExitStack

import concourse.mybir as mybir
from concourse.masks import make_identity

FP8X4 = mybir.dt.float8_e4m3fn_x4
BF16 = mybir.dt.bfloat16
F32 = mybir.dt.float32
I32 = mybir.dt.int32
U32 = mybir.dt.uint32
U8 = mybir.dt.uint8

P = 128
PACK = 4
TOKENS = 2 * 1024
D = 4096
EXPERTS = 8
RANK = 64
N_ALL = EXPERTS * RANK
PASSES = D // (P * PACK)
TILES = TOKENS // P
QUADS = 4
LANES = P // QUADS
D_QUAD = D // QUADS
PASSES_BANK = 2
BANKS_TILE = PASSES // PASSES_BANK
PSUM_BANKS = 8
HALF = PASSES // 2
X_BUFS = 8
HEAD = 4
STORE_TILES = 4
ON_VECTOR = ()

FLOPS = 2 * TOKENS * D * N_ALL


def tile_moelineara_e_kernel(tc, x, W_words, W_scales, *outs):
    nc = tc.nc

    x_rows = x.flatten_outer_dims()
    x_tiles = x_rows.rearrange("(m j) k -> m j k", j=TILES)
    x_lanes = x_rows.rearrange("(a b j) k -> j b a k", a=QUADS, b=LANES)
    out_tiles = [o.flatten_outer_dims().rearrange("(p j) r -> p j r", j=TILES) for o in outs]
    w_words_by_group = W_words.rearrange("(e c) p n t -> c p e (n t)", c=PASSES)
    w_scales_by_group = W_scales.rearrange("(e c) q n -> c q e n", c=PASSES)

    with ExitStack() as ctx:
        keep = ctx.enter_context(tc.tile_pool(name="keep", bufs=1))
        x_pool = ctx.enter_context(tc.tile_pool(name="x_pool", bufs=X_BUFS))
        sorted_pool = ctx.enter_context(tc.tile_pool(name="sorted_pool", bufs=4))
        turned_pool = ctx.enter_context(tc.tile_pool(name="turned_pool", bufs=1))
        grouped_pool = ctx.enter_context(tc.tile_pool(name="grouped_pool", bufs=3))
        quant_pool = ctx.enter_context(tc.tile_pool(name="quant_pool", bufs=HEAD + 2))
        res_pool = ctx.enter_context(tc.tile_pool(name="res_pool", bufs=TILES // STORE_TILES))
        psum = ctx.enter_context(tc.psum_pool(name="psum", bufs=PSUM_BANKS))
        ctx.enter_context(tc.manual_schedule())

        x_raw = {}
        x_sorted = {}
        x_turned = {}
        x_grouped = {}
        x_codes = {}
        x_planes = {}
        sums = {}
        results = {}

        def load_x(j):
            x_raw[j] = x_pool.tile([P, D], BF16, name="x_raw")
            if j in ON_VECTOR:
                load_quadrants(j, nc.sync, (0, 1))
            elif j < X_BUFS:
                for q in range(QUADS):
                    cols = slice(q * D_QUAD, (q + 1) * D_QUAD)
                    nc.sync.dma_start(out=x_raw[j][:, cols], in_=x_tiles[:, j, cols])
            else:
                nc.sync.dma_start(out=x_raw[j][:], in_=x_tiles[:, j, :])

        def load_quadrants(j, queue, quadrants):
            for q in quadrants:
                queue.dma_start(
                    out=x_raw[j][q * LANES : (q + 1) * LANES, :].rearrange("b (a k) -> b a k", a=QUADS),
                    in_=x_lanes[j][:, :, q * D_QUAD : (q + 1) * D_QUAD],
                )

        def sort_tile(j):
            x_sorted[j] = sorted_pool.tile([P, PASSES, 2, P], F32, name="x_sorted", align_bytes=64)
            if j < X_BUFS and j not in ON_VECTOR:
                words = x_raw[j][:].bitcast(F32).rearrange("p (s g i u) -> p s g u i", s=QUADS, g=PASSES, u=2)
                for s in range(QUADS):
                    nc.vector.tensor_copy(
                        out=x_sorted[j][:, :, :, s * LANES : (s + 1) * LANES],
                        in_=words[:, s],
                    )
            else:
                words = x_raw[j][:].bitcast(F32).rearrange("p (s g i u) -> p u g s i", s=QUADS, g=PASSES, u=2)
                for u in range(2):
                    nc.vector.tensor_copy(
                        out=x_sorted[j][:, :, u, :].rearrange("p g (s i) -> p g s i", s=QUADS),
                        in_=words[:, u],
                    )

        def sort_ahead(j):
            if j < TILES:
                sort_tile(j)
            if j + X_BUFS < TILES:
                load_x(j + X_BUFS)

        def new_grouped(j):
            x_grouped[j] = grouped_pool.tile([P, PASSES, P, PACK], BF16, name="grouped", align_bytes=64)
            return x_grouped[j][:].bitcast(F32)

        def transpose_tile(j):
            grouped_words = new_grouped(j)
            for b in range(BANKS_TILE):
                planes = psum.tile([P, PASSES_BANK, 2, P], F32, name="planes", tag="bank")
                for a in range(PASSES_BANK):
                    for u in range(2):
                        nc.tensor.transpose(
                            planes[:, a, u, :],
                            x_sorted[j][:, b * PASSES_BANK + a, u, :],
                            identity[:],
                        )
                nc.scalar.copy(
                    out=grouped_words[:, b * PASSES_BANK : (b + 1) * PASSES_BANK, :, :],
                    in_=planes[:].rearrange("p a u r -> p a r u"),
                )

        def turn_tile(j):
            x_turned[j] = turned_pool.tile([P, PASSES, 2, P], F32, name="turned", align_bytes=64)
            nc.vector.transpose(
                x_turned[j][:].rearrange("p g u r -> p (g u r)"),
                x_sorted[j][:].rearrange("p g u r -> p (g u r)"),
            )

        def interleave_tile(j):
            grouped_words = new_grouped(j)
            for h in range(2):
                some = slice(h * HALF, (h + 1) * HALF)
                nc.scalar.copy(
                    out=grouped_words[:, some, :, :],
                    in_=x_turned[j][:, some, :, :].rearrange("p g u r -> p g r u"),
                )

        def quantise_half(j, h):
            if h == 0:
                x_codes[j] = quant_pool.tile([P, PASSES, P], U32, name="x_codes", align_bytes=64)
                x_planes[j] = quant_pool.tile([P, PASSES, P], U8, name="x_planes", align_bytes=64)
            some = slice(h * HALF, (h + 1) * HALF)
            nc.vector.quantize_mx(
                out=x_codes[j][:, some, :].rearrange("p g r -> p (g r)").bitcast(FP8X4),
                scales=x_planes[j][:, some, :].rearrange("p g r -> p (g r)"),
                in_=x_grouped[j][:, some, :, :].rearrange("p g r t -> p (g r t)"),
            )

        def quantise_tile(j):
            quantise_half(j, 0)
            quantise_half(j, 1)

        def multiply_tiles(tiles):
            for j in tiles:
                sums[j] = psum.tile([P, N_ALL], F32, name="sums", tag="bank")
            for g in range(PASSES):
                for j in tiles:
                    nc.tensor.matmul_mx(
                        out=sums[j][:],
                        lhsT=x_codes[j][:, g, :].bitcast(FP8X4),
                        lhsT_scale=x_planes[j][:, g, :],
                        rhs=w_codes[:, g, :].bitcast(FP8X4),
                        rhs_scale=w_planes[PACK * (g % HALF) : P, g // HALF, :],
                        start=(g == 0),
                        stop=(g == PASSES - 1),
                    )

        def store_tile(j, on_vector=False):
            group, i = divmod(j, STORE_TILES)
            if i == 0:
                results[group] = res_pool.tile([P, EXPERTS, STORE_TILES, RANK], F32, name="results")
            copy = nc.vector.tensor_copy if on_vector else nc.scalar.copy
            copy(
                out=results[group][:, :, i, :],
                in_=sums[j][:].rearrange("p (e r) -> p e r", e=EXPERTS),
            )
            if i == STORE_TILES - 1 or j == TILES - 2:
                first = i if j == TILES - 1 else 0
                for e in range(EXPERTS):
                    nc.sync.dma_start(
                        out=out_tiles[e][:, group * STORE_TILES + first : j + 1, :],
                        in_=results[group][:, e, first : i + 1, :],
                    )

        def multiply_and_store(tiles):
            for i in tiles:
                multiply_tiles([i])
            for i in tiles:
                store_tile(i)

        identity = keep.tile([P, P], F32, name="identity")
        make_identity(nc, identity[:])

        for j in range(HEAD):
            load_x(j)

        w_planes = keep.tile([P, 2, N_ALL], U8, name="w_planes", align_bytes=64)
        nc.vector.memset(w_planes[:].bitcast(I32), 0)
        for q in range(QUADS):
            for c in range(2):
                nc.sync.dma_start(
                    out=w_planes[q * LANES : q * LANES + 16, c, :].bitcast(I32).rearrange("q (e n) -> q e n", e=EXPERTS),
                    in_=w_scales_by_group[2 * q + c].bitcast(I32),
                )
        w_codes = keep.tile([P, PASSES, N_ALL], U32, name="w_codes", align_bytes=64)
        for g in range(PASSES):
            for q in (0, 2, 1, 3):
                first = LANES * (g % HALF)
                nc.sync.dma_start(
                    out=w_codes[q * LANES : (q + 1) * LANES, g, :].bitcast(I32).rearrange("p (e n) -> p e n", e=EXPERTS),
                    in_=w_words_by_group[2 * q + g // HALF][first : first + LANES].bitcast(I32),
                )

        for j in range(HEAD, X_BUFS):
            load_x(j)

        sort_ahead(0)
        sort_ahead(1)
        for j in range(HEAD):
            transpose_tile(j)
            if j + 2 < HEAD:
                sort_ahead(j + 2)
            quantise_tile(j)
        sort_ahead(4)
        sort_ahead(5)
        multiply_tiles(list(range(HEAD)))
        for i in range(HEAD):
            store_tile(i)

        multiplied = HEAD
        for first in range(HEAD, TILES, 2):
            for j in range(first, first + 2):
                transpose_tile(j)
                quantise_tile(j)
                sort_ahead(j + 2)
            last = TILES if first + 2 == TILES else first + 1
            multiply_and_store(list(range(multiplied, last)))
            multiplied = last
